import numpy as np
import ml_dtypes


def mxq(x, axis, fmt="e4m3"):
    dtype, down = {"e4m3": (ml_dtypes.float8_e4m3fn, 7), "e5m2": (ml_dtypes.float8_e5m2, 14)}[fmt]
    v = np.moveaxis(np.asarray(x, np.float32).astype(ml_dtypes.bfloat16).astype(np.float64), axis, -1)
    blocks = v.reshape(v.shape[:-1] + (-1, 32))
    amax = np.abs(blocks).max(-1, keepdims=True)
    byte = np.maximum(np.where(amax > 0, np.frexp(amax)[1] - 1 + 127, 0) - down, 1)
    scale = np.exp2(byte - 127.0)
    codes = (blocks / scale).astype(np.float32).astype(dtype).astype(np.float64)
    return np.moveaxis((codes * scale).reshape(v.shape), -1, axis)


WIDE = False


def mx_kscale(k):
    if not WIDE:
        return np.ones(k)
    levels = np.array([10, -10, 5, -5, 0])
    a = np.random.permutation(np.resize(levels, k // 512 * 4)).reshape(k // 512, 4)
    idx = np.arange(k)
    return np.exp2(a[idx // 512, idx % 128 // 32])


BF16 = ml_dtypes.bfloat16


def bf(x):
    return np.asarray(x, np.float32).astype(BF16)


def f64(x):
    return np.asarray(x).astype(np.float64)


E2M1 = np.array([0.0, 0.5, 1.0, 1.5, 2.0, 3.0, 4.0, 6.0, -0.0, -0.5, -1.0, -1.5, -2.0, -3.0, -4.0, -6.0])


def pack_weight(w, fmt):
    k, n = w.shape
    w = f64(bf(w)).reshape(k // 32, 32, n)
    amax = np.abs(w).max(1)
    if fmt == "e4m3":
        byte = np.frexp(amax)[1] - 1 + 127 - 7
    else:
        mant, ex = np.frexp(amax / 6.0)
        byte = np.where(mant > 0.5, ex, ex - 1) + 127
    byte = np.clip(np.where(amax > 0, byte, 1), 1, 254)
    scaled = (w * np.exp2(127.0 - byte)[:, None, :]).reshape(k, n).astype(np.float32)
    by_word = np.ascontiguousarray(scaled.reshape(k // 512, 128, 4, n).transpose(0, 1, 3, 2))
    if fmt == "e4m3":
        words = by_word.astype(ml_dtypes.float8_e4m3fn).view(np.uint8)
    else:
        c = by_word.astype(ml_dtypes.float4_e2m1fn).view(np.uint8) & 0xF
        words = c[..., 0::2] | (c[..., 1::2] << 4)
    return np.ascontiguousarray(words), np.ascontiguousarray(byte.astype(np.uint8).reshape(k // 512, 16, n))


def unpack_weight(words, scales, fmt):
    g, p, n, _ = words.shape
    if fmt == "e4m3":
        vals = np.ascontiguousarray(words).view(ml_dtypes.float8_e4m3fn).astype(np.float64)
    else:
        nib = np.empty((g, p, n, 4), np.uint8)
        nib[..., 0::2] = words & 0xF
        nib[..., 1::2] = words >> 4
        vals = E2M1[nib]
    vals = vals * np.repeat(np.exp2(scales.astype(np.float64) - 127.0), 8, axis=1)[..., None]
    return vals.transpose(0, 1, 3, 2).reshape(g * 512, n)

def pack4(w):
    words, scales = pack_weight(w, "e2m1")
    return words.reshape(words.shape[0], 128, -1), scales


def unpack4(words, scales):
    return unpack_weight(words.reshape(words.shape[0], 128, -1, 2), scales, "e2m1")


T, HS, WS, WT, WH, WW, NH, HD, VID_DIM, TXT_DIM, TXT_LEN = 8, 8, 16, 8, 8, 8, 8, 128, 1536, 1536, 256
EPS = 1e-6
L_VID = T * HS * WS
N_WIN = (T // WT) * (HS // WH) * (WS // WW)
WIN_LEN = WT * WH * WW
INNER = NH * HD


def rmsnorm(x, gain):
    return x * (1.0 / np.sqrt(np.mean(x * x, axis=-1, keepdims=True) + EPS)) * gain


def window_partition(x):
    x = x.reshape(T // WT, WT, HS // WH, WH, WS // WW, WW, NH, HD)
    x = x.transpose(0, 2, 4, 1, 3, 5, 6, 7)
    return x.reshape(N_WIN, WIN_LEN, NH, HD)


def setup_inputs():
    s = mx_kscale(VID_DIM)
    vid = bf(np.random.standard_normal((L_VID, VID_DIM)) * s)
    words, scales = pack4(np.random.standard_normal((VID_DIM, 3 * INNER)) / np.sqrt(VID_DIM) / s[:, None])
    return {
        "vid": vid,
        "Wqkv_vid_words": words,
        "Wqkv_vid_scales": scales,
        "bqkv_vid": bf(0.1 * np.random.standard_normal(3 * INNER)),
        "q_scale_vid": bf(1.0 + 0.1 * np.random.standard_normal(HD)),
        "k_scale_vid": bf(1.0 + 0.1 * np.random.standard_normal(HD)),
    }


def reference(vid, Wqkv_vid_words, Wqkv_vid_scales, bqkv_vid, q_scale_vid, k_scale_vid):
    qkv = ((mxq(f64(vid), 1, "e4m3") @ unpack4(Wqkv_vid_words, Wqkv_vid_scales)) + f64(bqkv_vid)).reshape(L_VID, 3, NH, HD)
    q = rmsnorm(qkv[:, 0], f64(q_scale_vid))
    k = rmsnorm(qkv[:, 1], f64(k_scale_vid))
    return window_partition(q), window_partition(k), window_partition(qkv[:, 2])

@@ -1,0 +1,194 @@
+from contextlib import ExitStack
+
+import concourse.mybir as mybir
+from concourse.masks import make_identity
+
+F32 = mybir.dt.float32
+BF16 = mybir.dt.bfloat16
+I32 = mybir.dt.int32
+U32 = mybir.dt.uint32
+U8 = mybir.dt.uint8
+FP8X4 = mybir.dt.float8_e4m3fn_x4
+FP4X4 = mybir.dt.float4_e2m1fn_x4
+ALU = mybir.AluOpType
+ACT = mybir.ActivationFunctionType
+
+P = 128
+L_VID = 1024
+K = 1536
+K_PASS = 512
+PASSES = K // K_PASS
+HEADS = 8
+HD = 128
+INNER = HEADS * HD
+BANK = 512
+HALVES = INNER // BANK
+TOKEN_TILES = L_VID // P
+WINDOWS = 2
+TILES_PER_WINDOW = TOKEN_TILES // WINDOWS
+WIN_W = 8
+EPS = 1e-6
+
+FLOPS = 2 * L_VID * K * 3 * INNER
+
+
+def tile_naswinattention_pa_kernel(
+    tc, vid, w_words, w_scales, bias, q_gain, k_gain, out_q, out_k, out_v
+):
+    nc = tc.nc
+    outs = (out_q, out_k, out_v)
+    with ExitStack() as ctx:
+        ctx.enter_context(tc.manual_schedule())
+        keep = ctx.enter_context(tc.tile_pool(name="keep", bufs=1))
+        stage = ctx.enter_context(tc.tile_pool(name="stage", bufs=3))
+        work = ctx.enter_context(tc.tile_pool(name="work", bufs=4))
+        psum = ctx.enter_context(tc.psum_pool(name="psum", bufs=7))
+        psum_keep = ctx.enter_context(tc.psum_pool(name="psum_keep", bufs=1))
+
+        vectors = keep.tile([P, 3 * INNER + 2 * HD], BF16)
+        nc.vector.memset(vectors[:].bitcast(I32), 0)
+        nc.scalar.dma_start(out=vectors[0:1, 0 : 3 * INNER], in_=bias.unsqueeze(0))
+        nc.scalar.dma_start(out=vectors[0:1, 3 * INNER : 3 * INNER + HD], in_=q_gain.unsqueeze(0))
+        nc.scalar.dma_start(out=vectors[0:1, 3 * INNER + HD : 3 * INNER + 2 * HD], in_=k_gain.unsqueeze(0))
+        ones = keep.tile([P, P], BF16)
+        nc.vector.memset(ones[:], 1.0)
+        eps = keep.tile([P, 1], F32)
+        nc.vector.memset(eps[:], EPS)
+        ident = keep.tile([P, P], F32)
+        make_identity(nc, ident[:])
+        w_planes = keep.tile([P, PASSES, 3 * INNER], U8, align_bytes=64)
+        nc.vector.memset(w_planes[:].bitcast(I32), 0)
+
+        x_all = keep.tile([P, TOKEN_TILES, K], BF16)
+        vid_by_window = vid.rearrange("(a n b) k -> n a b k", n=WINDOWS, b=WIN_W)
+        runs = P // WIN_W
+        for m in range(TOKEN_TILES):
+            n, c = divmod(m, TILES_PER_WINDOW)
+            nc.sync.dma_start(out=x_all[:, m, :], in_=vid_by_window[n, runs * c : runs * (c + 1)])
+        scales_i32 = w_scales.bitcast(I32)
+        for quad in range(4):
+            nc.sync.dma_start(
+                out=w_planes[32 * quad : 32 * quad + 4].bitcast(I32),
+                in_=scales_i32[:, 4 * quad : 4 * quad + 4, :].rearrange("g r c -> r g c"),
+            )
+        w_codes = keep.tile([P, PASSES, 2 * 3 * INNER], U8, align_bytes=64)
+        words_i32 = w_words.bitcast(I32)
+        part_i32 = 2 * INNER // 4
+        for s in range(3):
+            cols = slice(part_i32 * s, part_i32 * (s + 1))
+            nc.sync.dma_start(
+                out=w_codes[:].bitcast(I32)[:, :, cols], in_=words_i32[:, :, cols].rearrange("g p c -> p g c")
+            )
+
+        x_codes = keep.tile([P, TOKEN_TILES * PASSES, P], U32, align_bytes=64)
+        x_planes = keep.tile([P, TOKEN_TILES * PASSES, P], U8, align_bytes=64)
+        units_per_bank = 2
+
+        def quantise(grouped, first):
+            units = slice(first, first + units_per_bank)
+            nc.vector.quantize_mx(
+                out=x_codes[:, units, :].rearrange("p i r -> p (i r)").bitcast(FP8X4),
+                scales=x_planes[:, units, :].rearrange("p i r -> p (i r)"),
+                in_=grouped[:].rearrange("p i r t -> p (i r t)"),
+            )
+
+        waiting = None
+        for first in range(0, TOKEN_TILES * PASSES, units_per_bank):
+            xt = psum.tile([P, units_per_bank, 2, P], F32, tag="bank")
+            for i in range(units_per_bank):
+                m, g = divmod(first + i, PASSES)
+                words = x_all[:, m, :].bitcast(F32)
+                for u in range(2):
+                    nc.tensor.transpose(xt[:, i, u, :], words[:, 256 * g + u : 256 * (g + 1) : 2], ident[:])
+            grouped = stage.tile([P, units_per_bank, P, 4], BF16, align_bytes=64)
+            source = xt[:].rearrange("p i u r -> p i r u")
+            if (first // units_per_bank) % 2 == 0:
+                nc.vector.tensor_copy(out=grouped[:].bitcast(F32), in_=source)
+            else:
+                nc.scalar.copy(out=grouped[:].bitcast(F32), in_=source)
+            if waiting is not None:
+                quantise(waiting[0], waiting[1])
+            waiting = (grouped, first)
+        quantise(waiting[0], waiting[1])
+
+        gain_bc = psum_keep.tile([P, 2, HD], F32)
+        nc.tensor.matmul(
+            out=gain_bc[:].rearrange("p s d -> p (s d)"),
+            lhsT=ones[:],
+            rhs=vectors[:, 3 * INNER : 3 * INNER + 2 * HD],
+            start=True,
+            stop=True,
+        )
+        bias_bc = keep.tile([P, 3 * INNER], F32)
+        for col0 in range(0, 3 * INNER, BANK):
+            spread = psum.tile([P, BANK], F32, tag="bank")
+            nc.tensor.matmul(out=spread[:], lhsT=ones[:], rhs=vectors[:, col0 : col0 + BANK], start=True, stop=True)
+            nc.scalar.copy(out=bias_bc[:, col0 : col0 + BANK], in_=spread[:])
+
+        def out_rows(m, s):
+            n, c = divmod(m, TILES_PER_WINDOW)
+            return outs[s][n, P * c : P * (c + 1)].rearrange("p h d -> p (h d)")
+
+        def project(m, s):
+            y = work.tile([P, INNER], F32, name="y")
+            for half in range(HALVES):
+                col0 = INNER * s + BANK * half
+                acc = psum.tile([P, BANK], F32, tag="bank", name="acc")
+                for g in range(PASSES):
+                    nc.tensor.matmul_mx(
+                        out=acc[:],
+                        lhsT=x_codes[:, PASSES * m + g, :].bitcast(FP8X4),
+                        lhsT_scale=x_planes[:, PASSES * m + g, :],
+                        rhs=w_codes[:, g, 2 * col0 : 2 * (col0 + BANK)].bitcast(FP4X4),
+                        rhs_scale=w_planes[:, g, col0 : col0 + BANK],
+                        start=(g == 0),
+                        stop=(g == PASSES - 1),
+                    )
+                y_half = y[:, BANK * half : BANK * (half + 1)]
+                bias_half = bias_bc[:, col0 : col0 + BANK]
+                if s == 2:
+                    nc.scalar.copy(out=y_half, in_=acc[:])
+                    nc.gpsimd.tensor_tensor(out=y_half, in0=y_half, in1=bias_half, op=ALU.add)
+                    nc.sync.dma_start(out=out_rows(m, s)[:, BANK * half : BANK * (half + 1)], in_=y_half)
+                else:
+                    nc.vector.tensor_tensor(out=y_half, in0=acc[:], in1=bias_half, op=ALU.add)
+            return y
+
+        def inverse_rms(y):
+            squares = work.tile([P, INNER], BF16, name="squares")
+            sumsq = work.tile([P, HEADS], F32, name="sumsq")
+            for h in range(HEADS):
+                head = slice(HD * h, HD * (h + 1))
+                nc.scalar.activation(
+                    out=squares[:, head], in_=y[:, head], func=ACT.Square, accum_out=sumsq[:, h : h + 1]
+                )
+            rstd = work.tile([P, HEADS], F32, name="rstd")
+            nc.scalar.activation(
+                out=rstd[:], in_=sumsq[:], func=ACT.Abs_reciprocal_sqrt, bias=eps[:, 0:1], scale=1.0 / HD
+            )
+            return rstd
+
+        def normalise_and_store(m, s, y, rstd):
+            normed = work.tile([P, INNER], F32, name="normed")
+            for h in range(HEADS):
+                head = slice(HD * h, HD * (h + 1))
+                nc.vector.scalar_tensor_tensor(
+                    out=normed[:, head],
+                    in0=y[:, head],
+                    scalar=rstd[:, h : h + 1],
+                    in1=gain_bc[:, s, :],
+                    op0=ALU.mult,
+                    op1=ALU.mult,
+                )
+            nc.sync.dma_start(out=out_rows(m, s), in_=normed[:])
+
+        waiting = None
+        for m in range(TOKEN_TILES):
+            for s in range(2):
+                y = project(m, s)
+                rstd = inverse_rms(y)
+                if waiting is not None:
+                    normalise_and_store(*waiting)
+                waiting = (m, s, y, rstd)
+            project(m, 2)
+        normalise_and_store(*waiting)

@@ -146,12 +146,9 @@ def tile_naswinattention_pa_kernel(
                     )
                 y_half = y[:, BANK * half : BANK * (half + 1)]
                 bias_half = bias_bc[:, col0 : col0 + BANK]
+                nc.vector.tensor_tensor(out=y_half, in0=acc[:], in1=bias_half, op=ALU.add)
                 if s == 2:
-                    nc.scalar.copy(out=y_half, in_=acc[:])
-                    nc.gpsimd.tensor_tensor(out=y_half, in0=y_half, in1=bias_half, op=ALU.add)
                     nc.sync.dma_start(out=out_rows(m, s)[:, BANK * half : BANK * (half + 1)], in_=y_half)
-                else:
-                    nc.vector.tensor_tensor(out=y_half, in0=acc[:], in1=bias_half, op=ALU.add)
             return y
 
         def inverse_rms(y):

@@ -28,6 +28,7 @@ WINDOWS = 2
 TILES_PER_WINDOW = TOKEN_TILES // WINDOWS
 WIN_W = 8
 EPS = 1e-6
+BANKS_OF_PASSES = ((0, 2), (2, 3))
 
 FLOPS = 2 * L_VID * K * 3 * INNER
 
@@ -40,76 +41,82 @@ def tile_naswinattention_pa_kernel(
     with ExitStack() as ctx:
         ctx.enter_context(tc.manual_schedule())
         keep = ctx.enter_context(tc.tile_pool(name="keep", bufs=1))
-        stage = ctx.enter_context(tc.tile_pool(name="stage", bufs=3))
-        work = ctx.enter_context(tc.tile_pool(name="work", bufs=4))
+        stage = ctx.enter_context(tc.tile_pool(name="stage", bufs=2))
+        work = ctx.enter_context(tc.tile_pool(name="work", bufs=6))
         psum = ctx.enter_context(tc.psum_pool(name="psum", bufs=7))
         psum_keep = ctx.enter_context(tc.psum_pool(name="psum_keep", bufs=1))
-
-        vectors = keep.tile([P, 3 * INNER + 2 * HD], BF16)
-        nc.vector.memset(vectors[:].bitcast(I32), 0)
-        nc.scalar.dma_start(out=vectors[0:1, 0 : 3 * INNER], in_=bias.unsqueeze(0))
-        nc.scalar.dma_start(out=vectors[0:1, 3 * INNER : 3 * INNER + HD], in_=q_gain.unsqueeze(0))
-        nc.scalar.dma_start(out=vectors[0:1, 3 * INNER + HD : 3 * INNER + 2 * HD], in_=k_gain.unsqueeze(0))
-        ones = keep.tile([P, P], BF16)
-        nc.vector.memset(ones[:], 1.0)
-        eps = keep.tile([P, 1], F32)
-        nc.vector.memset(eps[:], EPS)
-        ident = keep.tile([P, P], F32)
-        make_identity(nc, ident[:])
-        w_planes = keep.tile([P, PASSES, 3 * INNER], U8, align_bytes=64)
-        nc.vector.memset(w_planes[:].bitcast(I32), 0)
 
         x_all = keep.tile([P, TOKEN_TILES, K], BF16)
         vid_by_window = vid.rearrange("(a n b) k -> n a b k", n=WINDOWS, b=WIN_W)
         runs = P // WIN_W
-        for m in range(TOKEN_TILES):
+
+        def load_tokens(m):
             n, c = divmod(m, TILES_PER_WINDOW)
             nc.sync.dma_start(out=x_all[:, m, :], in_=vid_by_window[n, runs * c : runs * (c + 1)])
+
+        w_codes = keep.tile([P, PASSES, 2 * 3 * INNER], U8, align_bytes=64)
+        words_i32 = w_words.bitcast(I32)
+        part_i32 = 2 * INNER // 4
+
+        def load_words(s):
+            cols = slice(part_i32 * s, part_i32 * (s + 1))
+            nc.sync.dma_start(
+                out=w_codes[:].bitcast(I32)[:, :, cols], in_=words_i32[:, :, cols].rearrange("g p c -> p g c")
+            )
+
+        load_tokens(0)
+        load_words(0)
+        w_planes = keep.tile([P, PASSES, 3 * INNER], U8, align_bytes=64)
+        nc.vector.memset(w_planes[:].bitcast(I32), 0)
         scales_i32 = w_scales.bitcast(I32)
         for quad in range(4):
             nc.sync.dma_start(
                 out=w_planes[32 * quad : 32 * quad + 4].bitcast(I32),
                 in_=scales_i32[:, 4 * quad : 4 * quad + 4, :].rearrange("g r c -> r g c"),
             )
-        w_codes = keep.tile([P, PASSES, 2 * 3 * INNER], U8, align_bytes=64)
-        words_i32 = w_words.bitcast(I32)
-        part_i32 = 2 * INNER // 4
-        for s in range(3):
-            cols = slice(part_i32 * s, part_i32 * (s + 1))
-            nc.sync.dma_start(
-                out=w_codes[:].bitcast(I32)[:, :, cols], in_=words_i32[:, :, cols].rearrange("g p c -> p g c")
-            )
+        vectors = keep.tile([P, 3 * INNER + 2 * HD], BF16)
+        nc.gpsimd.memset(vectors[:].bitcast(F32), 0.0)
+        nc.scalar.dma_start(out=vectors[0:1, 0 : 3 * INNER], in_=bias.unsqueeze(0))
+        nc.scalar.dma_start(out=vectors[0:1, 3 * INNER : 3 * INNER + HD], in_=q_gain.unsqueeze(0))
+        nc.scalar.dma_start(out=vectors[0:1, 3 * INNER + HD : 3 * INNER + 2 * HD], in_=k_gain.unsqueeze(0))
+        load_tokens(1)
+        load_words(2)
+        load_words(1)
+        for m in range(2, TOKEN_TILES):
+            load_tokens(m)
+
+        ones = keep.tile([P, P], BF16)
+        nc.vector.memset(ones[:], 1.0)
+        eps = keep.tile([P, 1], F32)
+        nc.vector.memset(eps[:], EPS)
+        ident = keep.tile([P, P], F32)
+        make_identity(nc, ident[:])
 
         x_codes = keep.tile([P, TOKEN_TILES * PASSES, P], U32, align_bytes=64)
         x_planes = keep.tile([P, TOKEN_TILES * PASSES, P], U8, align_bytes=64)
-        units_per_bank = 2
 
-        def quantise(grouped, first):
-            units = slice(first, first + units_per_bank)
-            nc.vector.quantize_mx(
-                out=x_codes[:, units, :].rearrange("p i r -> p (i r)").bitcast(FP8X4),
-                scales=x_planes[:, units, :].rearrange("p i r -> p (i r)"),
-                in_=grouped[:].rearrange("p i r t -> p (i r t)"),
-            )
+        def transpose_tokens(m):
+            words = x_all[:, m, :].bitcast(F32)
+            grouped = stage.tile([P, PASSES, P, 4], BF16, align_bytes=64, name="grouped")
+            for g0, g1 in BANKS_OF_PASSES:
+                xt = psum.tile([P, g1 - g0, 2, P], F32, tag="bank", name="xt")
+                for g in range(g0, g1):
+                    for u in range(2):
+                        nc.tensor.transpose(xt[:, g - g0, u, :], words[:, 256 * g + u : 256 * (g + 1) : 2], ident[:])
+                nc.scalar.copy(out=grouped[:, g0:g1].bitcast(F32), in_=xt[:].rearrange("p i u r -> p i r u"))
+            return grouped
 
-        waiting = None
-        for first in range(0, TOKEN_TILES * PASSES, units_per_bank):
-            xt = psum.tile([P, units_per_bank, 2, P], F32, tag="bank")
-            for i in range(units_per_bank):
-                m, g = divmod(first + i, PASSES)
-                words = x_all[:, m, :].bitcast(F32)
-                for u in range(2):
-                    nc.tensor.transpose(xt[:, i, u, :], words[:, 256 * g + u : 256 * (g + 1) : 2], ident[:])
-            grouped = stage.tile([P, units_per_bank, P, 4], BF16, align_bytes=64)
-            source = xt[:].rearrange("p i u r -> p i r u")
-            if (first // units_per_bank) % 2 == 0:
-                nc.vector.tensor_copy(out=grouped[:].bitcast(F32), in_=source)
-            else:
-                nc.scalar.copy(out=grouped[:].bitcast(F32), in_=source)
-            if waiting is not None:
-                quantise(waiting[0], waiting[1])
-            waiting = (grouped, first)
-        quantise(waiting[0], waiting[1])
+        def quantise_tokens(m, grouped):
+            for g0, g1 in BANKS_OF_PASSES:
+                units = slice(PASSES * m + g0, PASSES * m + g1)
+                nc.vector.quantize_mx(
+                    out=x_codes[:, units, :].rearrange("p i r -> p (i r)").bitcast(FP8X4),
+                    scales=x_planes[:, units, :].rearrange("p i r -> p (i r)"),
+                    in_=grouped[:, g0:g1].rearrange("p i r t -> p (i r t)"),
+                )
+
+        grouped = transpose_tokens(0)
+        quantise_tokens(0, grouped)
 
         gain_bc = psum_keep.tile([P, 2, HD], F32)
         nc.tensor.matmul(
@@ -146,9 +153,12 @@ def tile_naswinattention_pa_kernel(
                     )
                 y_half = y[:, BANK * half : BANK * (half + 1)]
                 bias_half = bias_bc[:, col0 : col0 + BANK]
-                nc.vector.tensor_tensor(out=y_half, in0=acc[:], in1=bias_half, op=ALU.add)
                 if s == 2:
+                    nc.scalar.copy(out=y_half, in_=acc[:])
+                    nc.gpsimd.tensor_tensor(out=y_half, in0=y_half, in1=bias_half, op=ALU.add)
                     nc.sync.dma_start(out=out_rows(m, s)[:, BANK * half : BANK * (half + 1)], in_=y_half)
+                else:
+                    nc.vector.tensor_tensor(out=y_half, in0=acc[:], in1=bias_half, op=ALU.add)
             return y
 
         def inverse_rms(y):
@@ -166,26 +176,32 @@ def tile_naswinattention_pa_kernel(
             return rstd
 
         def normalise_and_store(m, s, y, rstd):
-            normed = work.tile([P, INNER], F32, name="normed")
-            for h in range(HEADS):
-                head = slice(HD * h, HD * (h + 1))
-                nc.vector.scalar_tensor_tensor(
-                    out=normed[:, head],
-                    in0=y[:, head],
-                    scalar=rstd[:, h : h + 1],
-                    in1=gain_bc[:, s, :],
-                    op0=ALU.mult,
-                    op1=ALU.mult,
-                )
-            nc.sync.dma_start(out=out_rows(m, s), in_=normed[:])
+            heads_per_bank = BANK // HD
+            for half in range(HALVES):
+                normed = work.tile([P, BANK], F32, name="normed")
+                for i in range(heads_per_bank):
+                    h = heads_per_bank * half + i
+                    nc.vector.scalar_tensor_tensor(
+                        out=normed[:, HD * i : HD * (i + 1)],
+                        in0=y[:, HD * h : HD * (h + 1)],
+                        scalar=rstd[:, h : h + 1],
+                        in1=gain_bc[:, s, :],
+                        op0=ALU.mult,
+                        op1=ALU.mult,
+                    )
+                nc.sync.dma_start(out=out_rows(m, s)[:, BANK * half : BANK * (half + 1)], in_=normed[:])
 
-        waiting = None
         for m in range(TOKEN_TILES):
-            for s in range(2):
-                y = project(m, s)
-                rstd = inverse_rms(y)
-                if waiting is not None:
-                    normalise_and_store(*waiting)
-                waiting = (m, s, y, rstd)
+            q = project(m, 0)
+            q_rstd = inverse_rms(q)
+            if m > 0:
+                normalise_and_store(m - 1, 1, k, k_rstd)
+            if m + 1 < TOKEN_TILES:
+                grouped = transpose_tokens(m + 1)
             project(m, 2)
-        normalise_and_store(*waiting)
+            if m + 1 < TOKEN_TILES:
+                quantise_tokens(m + 1, grouped)
+            k = project(m, 1)
+            k_rstd = inverse_rms(k)
+            normalise_and_store(m, 0, q, q_rstd)
+        normalise_and_store(TOKEN_TILES - 1, 1, k, k_rstd)

@@ -141,7 +141,7 @@ def tile_naswinattention_pa_kernel(
             for half in range(HALVES):
                 col0 = INNER * s + BANK * half
                 acc = psum.tile([P, BANK], F32, tag="bank", name="acc")
-                for g in range(PASSES):
+                for g in 2 * tuple(range(PASSES)):
                     nc.tensor.matmul_mx(
                         out=acc[:],
                         lhsT=x_codes[:, PASSES * m + g, :].bitcast(FP8X4),

@@ -64,7 +64,13 @@ def tile_naswinattention_pa_kernel(
                 out=w_codes[:].bitcast(I32)[:, :, cols], in_=words_i32[:, :, cols].rearrange("g p c -> p g c")
             )
 
+        vectors = keep.tile([P, 3 * INNER + 2 * HD], BF16)
+        nc.gpsimd.memset(vectors[:].bitcast(F32), 0.0)
+        nc.scalar.dma_start(out=vectors[0:1, 0 : 3 * INNER], in_=bias.unsqueeze(0))
+        nc.scalar.dma_start(out=vectors[0:1, 3 * INNER : 3 * INNER + HD], in_=q_gain.unsqueeze(0))
+        nc.scalar.dma_start(out=vectors[0:1, 3 * INNER + HD : 3 * INNER + 2 * HD], in_=k_gain.unsqueeze(0))
         load_tokens(0)
+        load_tokens(1)
         load_words(0)
         w_planes = keep.tile([P, PASSES, 3 * INNER], U8, align_bytes=64)
         nc.vector.memset(w_planes[:].bitcast(I32), 0)
@@ -74,12 +80,6 @@ def tile_naswinattention_pa_kernel(
                 out=w_planes[32 * quad : 32 * quad + 4].bitcast(I32),
                 in_=scales_i32[:, 4 * quad : 4 * quad + 4, :].rearrange("g r c -> r g c"),
             )
-        vectors = keep.tile([P, 3 * INNER + 2 * HD], BF16)
-        nc.gpsimd.memset(vectors[:].bitcast(F32), 0.0)
-        nc.scalar.dma_start(out=vectors[0:1, 0 : 3 * INNER], in_=bias.unsqueeze(0))
-        nc.scalar.dma_start(out=vectors[0:1, 3 * INNER : 3 * INNER + HD], in_=q_gain.unsqueeze(0))
-        nc.scalar.dma_start(out=vectors[0:1, 3 * INNER + HD : 3 * INNER + 2 * HD], in_=k_gain.unsqueeze(0))
-        load_tokens(1)
         load_words(2)
         load_words(1)
         for m in range(2, TOKEN_TILES):
@@ -141,7 +141,7 @@ def tile_naswinattention_pa_kernel(
             for half in range(HALVES):
                 col0 = INNER * s + BANK * half
                 acc = psum.tile([P, BANK], F32, tag="bank", name="acc")
-                for g in 2 * tuple(range(PASSES)):
+                for g in range(PASSES):
                     nc.tensor.matmul_mx(
                         out=acc[:],
                         lhsT=x_codes[:, PASSES * m + g, :].bitcast(FP8X4),
@@ -153,12 +153,13 @@ def tile_naswinattention_pa_kernel(
                     )
                 y_half = y[:, BANK * half : BANK * (half + 1)]
                 bias_half = bias_bc[:, col0 : col0 + BANK]
-                if s == 2:
+                if s == 2 and half == 1:
                     nc.scalar.copy(out=y_half, in_=acc[:])
                     nc.gpsimd.tensor_tensor(out=y_half, in0=y_half, in1=bias_half, op=ALU.add)
-                    nc.sync.dma_start(out=out_rows(m, s)[:, BANK * half : BANK * (half + 1)], in_=y_half)
                 else:
                     nc.vector.tensor_tensor(out=y_half, in0=acc[:], in1=bias_half, op=ALU.add)
+                if s == 2:
+                    nc.sync.dma_start(out=out_rows(m, s)[:, BANK * half : BANK * (half + 1)], in_=y_half)
             return y
 
         def inverse_rms(y):
@@ -192,12 +193,12 @@ def tile_naswinattention_pa_kernel(
                 nc.sync.dma_start(out=out_rows(m, s)[:, BANK * half : BANK * (half + 1)], in_=normed[:])
 
         for m in range(TOKEN_TILES):
+            if m + 1 < TOKEN_TILES:
+                grouped = transpose_tokens(m + 1)
             q = project(m, 0)
             q_rstd = inverse_rms(q)
             if m > 0:
                 normalise_and_store(m - 1, 1, k, k_rstd)
-            if m + 1 < TOKEN_TILES:
-                grouped = transpose_tokens(m + 1)
             project(m, 2)
             if m + 1 < TOKEN_TILES:
                 quantise_tokens(m + 1, grouped)

@@ -23,12 +23,18 @@ HD = 128
 INNER = HEADS * HD
 BANK = 512
 HALVES = INNER // BANK
+BANK_HEADS = BANK // HD
 TOKEN_TILES = L_VID // P
 WINDOWS = 2
 TILES_PER_WINDOW = TOKEN_TILES // WINDOWS
 WIN_W = 8
 EPS = 1e-6
-BANKS_OF_PASSES = ((0, 2), (2, 3))
+Q, KK, V = 0, 1, 2
+PAIR = 2
+BLOCKS = TOKEN_TILES // PAIR
+UNITS = PAIR * PASSES
+UNIT_BANKS = UNITS // 2
+LAG = 2
 
 FLOPS = 2 * L_VID * K * 3 * INNER
 
@@ -41,12 +47,42 @@ def tile_naswinattention_pa_kernel(
     with ExitStack() as ctx:
         ctx.enter_context(tc.manual_schedule())
         keep = ctx.enter_context(tc.tile_pool(name="keep", bufs=1))
-        stage = ctx.enter_context(tc.tile_pool(name="stage", bufs=2))
-        work = ctx.enter_context(tc.tile_pool(name="work", bufs=6))
+        stage = ctx.enter_context(tc.tile_pool(name="stage", bufs=4))
+        sums = ctx.enter_context(tc.tile_pool(name="sums", bufs=10))
+        results = ctx.enter_context(tc.tile_pool(name="results", bufs=6))
+        junk = ctx.enter_context(tc.tile_pool(name="junk", bufs=2))
         psum = ctx.enter_context(tc.psum_pool(name="psum", bufs=7))
         psum_keep = ctx.enter_context(tc.psum_pool(name="psum_keep", bufs=1))
 
         x_all = keep.tile([P, TOKEN_TILES, K], BF16)
+        w_codes = {
+            Q: [keep.tile([P, PASSES, 2 * BANK], U8, align_bytes=64, name="codes_q%d" % half) for half in range(HALVES)],
+            KK: [keep.tile([P, PASSES, 2 * INNER], U8, align_bytes=64, name="codes_k")],
+            V: [keep.tile([P, PASSES, 2 * INNER], U8, align_bytes=64, name="codes_v")],
+        }
+        w_planes = [keep.tile([P, PASSES, INNER], U8, align_bytes=64, name="planes%d" % s) for s in (Q, KK, V)]
+        first_rows = keep.tile([P, INNER + 2 * HD], BF16)
+        later_rows = keep.tile([P, 2 * INNER], BF16)
+        ones = keep.tile([P, P], BF16)
+        eps = keep.tile([P, 1], F32)
+        warm = keep.tile([P, 1], F32)
+        ident = keep.tile([P, P], F32)
+        bias_bc = keep.tile([P, 3, INNER], BF16)
+        x_codes = keep.tile([P, TOKEN_TILES * PASSES, P], U32, align_bytes=64)
+        x_planes = keep.tile([P, TOKEN_TILES * PASSES, P], U8, align_bytes=64)
+
+        def zero_planes(s):
+            nc.vector.memset(w_planes[s][:].bitcast(I32), 0)
+
+        nc.gpsimd.memset(first_rows[:].bitcast(F32), 0.0)
+        make_identity(nc, ident[:])
+        nc.gpsimd.memset(later_rows[:].bitcast(F32), 0.0)
+        nc.vector.memset(eps[:], EPS)
+        zero_planes(Q)
+        nc.vector.memset(ones[:], 1.0)
+        zero_planes(KK)
+        zero_planes(V)
+
         vid_by_window = vid.rearrange("(a n b) k -> n a b k", n=WINDOWS, b=WIN_W)
         runs = P // WIN_W
 
@@ -54,155 +90,203 @@ def tile_naswinattention_pa_kernel(
             n, c = divmod(m, TILES_PER_WINDOW)
             nc.sync.dma_start(out=x_all[:, m, :], in_=vid_by_window[n, runs * c : runs * (c + 1)])
 
-        w_codes = keep.tile([P, PASSES, 2 * 3 * INNER], U8, align_bytes=64)
         words_i32 = w_words.bitcast(I32)
-        part_i32 = 2 * INNER // 4
+        part_words = 2 * INNER // 4
 
         def load_words(s):
-            cols = slice(part_i32 * s, part_i32 * (s + 1))
-            nc.sync.dma_start(
-                out=w_codes[:].bitcast(I32)[:, :, cols], in_=words_i32[:, :, cols].rearrange("g p c -> p g c")
-            )
+            width = part_words // len(w_codes[s])
+            for i, codes in enumerate(w_codes[s]):
+                cols = slice(part_words * s + width * i, part_words * s + width * (i + 1))
+                nc.sync.dma_start(out=codes[:].bitcast(I32), in_=words_i32[:, :, cols].rearrange("g p c -> p g c"))
 
-        vectors = keep.tile([P, 3 * INNER + 2 * HD], BF16)
-        nc.gpsimd.memset(vectors[:].bitcast(F32), 0.0)
-        nc.scalar.dma_start(out=vectors[0:1, 0 : 3 * INNER], in_=bias.unsqueeze(0))
-        nc.scalar.dma_start(out=vectors[0:1, 3 * INNER : 3 * INNER + HD], in_=q_gain.unsqueeze(0))
-        nc.scalar.dma_start(out=vectors[0:1, 3 * INNER + HD : 3 * INNER + 2 * HD], in_=k_gain.unsqueeze(0))
-        load_tokens(0)
-        load_tokens(1)
-        load_words(0)
-        w_planes = keep.tile([P, PASSES, 3 * INNER], U8, align_bytes=64)
-        nc.vector.memset(w_planes[:].bitcast(I32), 0)
         scales_i32 = w_scales.bitcast(I32)
-        for quad in range(4):
-            nc.sync.dma_start(
-                out=w_planes[32 * quad : 32 * quad + 4].bitcast(I32),
-                in_=scales_i32[:, 4 * quad : 4 * quad + 4, :].rearrange("g r c -> r g c"),
-            )
-        load_words(2)
-        load_words(1)
-        for m in range(2, TOKEN_TILES):
-            load_tokens(m)
+        part_i32 = INNER // 4
 
-        ones = keep.tile([P, P], BF16)
-        nc.vector.memset(ones[:], 1.0)
-        eps = keep.tile([P, 1], F32)
-        nc.vector.memset(eps[:], EPS)
-        ident = keep.tile([P, P], F32)
-        make_identity(nc, ident[:])
-
-        x_codes = keep.tile([P, TOKEN_TILES * PASSES, P], U32, align_bytes=64)
-        x_planes = keep.tile([P, TOKEN_TILES * PASSES, P], U8, align_bytes=64)
-
-        def transpose_tokens(m):
-            words = x_all[:, m, :].bitcast(F32)
-            grouped = stage.tile([P, PASSES, P, 4], BF16, align_bytes=64, name="grouped")
-            for g0, g1 in BANKS_OF_PASSES:
-                xt = psum.tile([P, g1 - g0, 2, P], F32, tag="bank", name="xt")
-                for g in range(g0, g1):
-                    for u in range(2):
-                        nc.tensor.transpose(xt[:, g - g0, u, :], words[:, 256 * g + u : 256 * (g + 1) : 2], ident[:])
-                nc.scalar.copy(out=grouped[:, g0:g1].bitcast(F32), in_=xt[:].rearrange("p i u r -> p i r u"))
-            return grouped
-
-        def quantise_tokens(m, grouped):
-            for g0, g1 in BANKS_OF_PASSES:
-                units = slice(PASSES * m + g0, PASSES * m + g1)
-                nc.vector.quantize_mx(
-                    out=x_codes[:, units, :].rearrange("p i r -> p (i r)").bitcast(FP8X4),
-                    scales=x_planes[:, units, :].rearrange("p i r -> p (i r)"),
-                    in_=grouped[:, g0:g1].rearrange("p i r t -> p (i r t)"),
+        def load_scales(s):
+            for quad in range(4):
+                nc.sync.dma_start(
+                    out=w_planes[s][32 * quad : 32 * quad + 4].bitcast(I32),
+                    in_=scales_i32[:, 4 * quad : 4 * quad + 4, part_i32 * s : part_i32 * (s + 1)].rearrange(
+                        "g r c -> r g c"
+                    ),
                 )
 
-        grouped = transpose_tokens(0)
-        quantise_tokens(0, grouped)
+        bias_row = bias.unsqueeze(0)
+        nc.scalar.dma_start(out=first_rows[0:1, 0:INNER], in_=bias_row[:, 0:INNER])
+        nc.scalar.dma_start(out=first_rows[0:1, INNER : INNER + HD], in_=q_gain.unsqueeze(0))
+        nc.scalar.dma_start(out=first_rows[0:1, INNER + HD : INNER + 2 * HD], in_=k_gain.unsqueeze(0))
+        nc.scalar.dma_start(out=later_rows[0:1, :], in_=bias_row[:, INNER : 3 * INNER])
+        nc.scalar.activation(out=warm[:], in_=eps[:], func=ACT.Abs_reciprocal_sqrt)
+        load_tokens(0)
+        load_tokens(1)
+        load_scales(Q)
+        load_words(Q)
+        load_tokens(2)
+        load_tokens(3)
+        load_scales(KK)
+        load_words(KK)
+        load_scales(V)
+        load_words(V)
+        for m in range(4, TOKEN_TILES):
+            load_tokens(m)
 
-        gain_bc = psum_keep.tile([P, 2, HD], F32)
-        nc.tensor.matmul(
-            out=gain_bc[:].rearrange("p s d -> p (s d)"),
-            lhsT=ones[:],
-            rhs=vectors[:, 3 * INNER : 3 * INNER + 2 * HD],
-            start=True,
-            stop=True,
-        )
-        bias_bc = keep.tile([P, 3 * INNER], F32)
-        for col0 in range(0, 3 * INNER, BANK):
-            spread = psum.tile([P, BANK], F32, tag="bank")
-            nc.tensor.matmul(out=spread[:], lhsT=ones[:], rhs=vectors[:, col0 : col0 + BANK], start=True, stop=True)
-            nc.scalar.copy(out=bias_bc[:, col0 : col0 + BANK], in_=spread[:])
+        def transpose_units(first):
+            xt = psum.tile([P, 2, 2, P], F32, tag="bank", name="xt")
+            for i in range(2):
+                m, g = divmod(first + i, PASSES)
+                words = x_all[:, m, :].bitcast(F32)
+                for u in range(2):
+                    nc.tensor.transpose(xt[:, i, u, :], words[:, 256 * g + u : 256 * (g + 1) : 2], ident[:])
+            return xt
 
-        def out_rows(m, s):
-            n, c = divmod(m, TILES_PER_WINDOW)
-            return outs[s][n, P * c : P * (c + 1)].rearrange("p h d -> p (h d)")
+        def group_units(xt):
+            grouped = stage.tile([P, 2, P, 4], BF16, align_bytes=64, name="grouped")
+            nc.scalar.copy(out=grouped[:].bitcast(F32), in_=xt[:].rearrange("p i u r -> p i r u"))
+            return grouped
 
-        def project(m, s):
-            y = work.tile([P, INNER], F32, name="y")
+        def quantise_units(first, grouped):
+            nc.vector.quantize_mx(
+                out=x_codes[:, first : first + 2, :].rearrange("p i r -> p (i r)").bitcast(FP8X4),
+                scales=x_planes[:, first : first + 2, :].rearrange("p i r -> p (i r)"),
+                in_=grouped[:].rearrange("p i r t -> p (i r t)"),
+            )
+
+        def spread_bias(s, engine_copy):
+            spread = psum.tile([P, INNER], BF16, tag="bank", name="spread")
             for half in range(HALVES):
-                col0 = INNER * s + BANK * half
-                acc = psum.tile([P, BANK], F32, tag="bank", name="acc")
-                for g in range(PASSES):
-                    nc.tensor.matmul_mx(
-                        out=acc[:],
-                        lhsT=x_codes[:, PASSES * m + g, :].bitcast(FP8X4),
-                        lhsT_scale=x_planes[:, PASSES * m + g, :],
-                        rhs=w_codes[:, g, 2 * col0 : 2 * (col0 + BANK)].bitcast(FP4X4),
-                        rhs_scale=w_planes[:, g, col0 : col0 + BANK],
-                        start=(g == 0),
-                        stop=(g == PASSES - 1),
-                    )
-                y_half = y[:, BANK * half : BANK * (half + 1)]
-                bias_half = bias_bc[:, col0 : col0 + BANK]
-                if s == 2 and half == 1:
-                    nc.scalar.copy(out=y_half, in_=acc[:])
-                    nc.gpsimd.tensor_tensor(out=y_half, in0=y_half, in1=bias_half, op=ALU.add)
-                else:
-                    nc.vector.tensor_tensor(out=y_half, in0=acc[:], in1=bias_half, op=ALU.add)
-                if s == 2:
-                    nc.sync.dma_start(out=out_rows(m, s)[:, BANK * half : BANK * (half + 1)], in_=y_half)
+                cols = slice(BANK * half, BANK * (half + 1))
+                nc.tensor.matmul(
+                    out=spread[:, cols],
+                    lhsT=ones[:],
+                    rhs=(first_rows if s == Q else later_rows)[:, INNER * max(s - 1, 0) + BANK * half :][:, 0:BANK],
+                    start=True,
+                    stop=True,
+                )
+            engine_copy(out=bias_bc[:, s, :], in_=spread[:])
+
+        def out_rows(m, s, half):
+            n, c = divmod(m, TILES_PER_WINDOW)
+            return outs[s][n, P * c : P * (c + 1)].rearrange("p h d -> p (h d)")[:, BANK * half : BANK * (half + 1)]
+
+        def multiply(m, s, half):
+            col0 = BANK * half
+            tiles_of_part = len(w_codes[s])
+            codes = w_codes[s][half * tiles_of_part // HALVES]
+            code0 = 2 * col0 % (2 * INNER // tiles_of_part)
+            acc = psum.tile([P, BANK], F32, tag="bank", name="acc")
+            for g in range(PASSES):
+                nc.tensor.matmul_mx(
+                    out=acc[:],
+                    lhsT=x_codes[:, PASSES * m + g, :].bitcast(FP8X4),
+                    lhsT_scale=x_planes[:, PASSES * m + g, :],
+                    rhs=codes[:, g, code0 : code0 + 2 * BANK].bitcast(FP4X4),
+                    rhs_scale=w_planes[s][:, g, col0 : col0 + BANK],
+                    start=(g == 0),
+                    stop=(g == PASSES - 1),
+                )
+            return acc
+
+        def bias_of(s, half):
+            return bias_bc[:, s, BANK * half : BANK * (half + 1)]
+
+        def add_bias(acc, s, half):
+            y = sums.tile([P, BANK], F32, name="y")
+            nc.vector.tensor_tensor(out=y[:], in0=acc[:], in1=bias_of(s, half), op=ALU.add)
             return y
 
         def inverse_rms(y):
-            squares = work.tile([P, INNER], BF16, name="squares")
-            sumsq = work.tile([P, HEADS], F32, name="sumsq")
-            for h in range(HEADS):
+            squares = junk.tile([P, BANK], BF16, name="squares")
+            sumsq = sums.tile([P, BANK_HEADS], F32, name="sumsq")
+            for h in range(BANK_HEADS):
                 head = slice(HD * h, HD * (h + 1))
                 nc.scalar.activation(
                     out=squares[:, head], in_=y[:, head], func=ACT.Square, accum_out=sumsq[:, h : h + 1]
                 )
-            rstd = work.tile([P, HEADS], F32, name="rstd")
+            rstd = sums.tile([P, BANK_HEADS], F32, name="rstd")
             nc.scalar.activation(
                 out=rstd[:], in_=sumsq[:], func=ACT.Abs_reciprocal_sqrt, bias=eps[:, 0:1], scale=1.0 / HD
             )
             return rstd
 
-        def normalise_and_store(m, s, y, rstd):
-            heads_per_bank = BANK // HD
-            for half in range(HALVES):
-                normed = work.tile([P, BANK], F32, name="normed")
-                for i in range(heads_per_bank):
-                    h = heads_per_bank * half + i
-                    nc.vector.scalar_tensor_tensor(
-                        out=normed[:, HD * i : HD * (i + 1)],
-                        in0=y[:, HD * h : HD * (h + 1)],
-                        scalar=rstd[:, h : h + 1],
-                        in1=gain_bc[:, s, :],
-                        op0=ALU.mult,
-                        op1=ALU.mult,
-                    )
-                nc.sync.dma_start(out=out_rows(m, s)[:, BANK * half : BANK * (half + 1)], in_=normed[:])
+        def normalise_and_store(m, s, half, y, rstd):
+            normed = results.tile([P, BANK], F32, name="normed")
+            for h in range(BANK_HEADS):
+                head = slice(HD * h, HD * (h + 1))
+                nc.vector.scalar_tensor_tensor(
+                    out=normed[:, head],
+                    in0=y[:, head],
+                    scalar=rstd[:, h : h + 1],
+                    in1=gain_bc[:, s, :],
+                    op0=ALU.mult,
+                    op1=ALU.mult,
+                )
+            nc.sync.dma_start(out=out_rows(m, s, half), in_=normed[:])
 
-        for m in range(TOKEN_TILES):
-            if m + 1 < TOKEN_TILES:
-                grouped = transpose_tokens(m + 1)
-            q = project(m, 0)
-            q_rstd = inverse_rms(q)
-            if m > 0:
-                normalise_and_store(m - 1, 1, k, k_rstd)
-            project(m, 2)
-            if m + 1 < TOKEN_TILES:
-                quantise_tokens(m + 1, grouped)
-            k = project(m, 1)
-            k_rstd = inverse_rms(k)
-            normalise_and_store(m, 0, q, q_rstd)
-        normalise_and_store(TOKEN_TILES - 1, 1, k, k_rstd)
+        def normalise_banks(waiting, done, upto):
+            for entry in waiting[done:upto]:
+                normalise_and_store(*entry)
+            return max(done, upto)
+
+        def v_on_vector(m, half, acc):
+            value = results.tile([P, BANK], F32, name="value")
+            nc.vector.tensor_tensor(out=value[:], in0=acc[:], in1=bias_of(V, half), op=ALU.add)
+            nc.sync.dma_start(out=out_rows(m, V, half), in_=value[:])
+
+        def v_leaves_psum(acc):
+            value = results.tile([P, BANK], F32, name="value")
+            nc.scalar.copy(out=value[:], in_=acc[:])
+            return value
+
+        def v_on_gpsimd(m, half, value):
+            nc.gpsimd.tensor_tensor(out=value[:], in0=value[:], in1=bias_of(V, half), op=ALU.add)
+            nc.sync.dma_start(out=out_rows(m, V, half), in_=value[:])
+
+        banks = [transpose_units(2 * c) for c in range(UNIT_BANKS)]
+        for c in range(UNIT_BANKS):
+            quantise_units(2 * c, group_units(banks[c]))
+        gain_bc = psum_keep.tile([P, 2, HD], F32)
+        nc.tensor.matmul(
+            out=gain_bc[:].rearrange("p s d -> p (s d)"),
+            lhsT=ones[:],
+            rhs=first_rows[:, INNER : INNER + 2 * HD],
+            start=True,
+            stop=True,
+        )
+        spread_bias(Q, nc.vector.tensor_copy)
+
+        for j in range(BLOCKS):
+            tiles = (PAIR * j, PAIR * j + 1)
+            last = j == BLOCKS - 1
+            waiting = []
+            done = 0
+            for s in (Q, KK):
+                if s == KK and not last:
+                    done = normalise_banks(waiting, done, len(waiting))
+                    banks = [transpose_units(UNITS * (j + 1) + 2 * c) for c in range(UNIT_BANKS)]
+                    grouped = [group_units(xt) for xt in banks]
+                if s == KK and j == 0:
+                    spread_bias(KK, nc.vector.tensor_copy)
+                    spread_bias(V, nc.scalar.copy)
+                for i, (m, half) in enumerate([(m, half) for m in tiles for half in range(HALVES)]):
+                    y = add_bias(multiply(m, s, half), s, half)
+                    waiting.append((m, s, half, y, inverse_rms(y)))
+                    done = normalise_banks(waiting, done, len(waiting) - LAG)
+                    if s == KK and not last and i < UNIT_BANKS:
+                        quantise_units(UNITS * (j + 1) + 2 * i, grouped[i])
+            if not last:
+                done = normalise_banks(waiting, done, len(waiting))
+                values = [
+                    (m, half, v_leaves_psum(multiply(m, V, half)))
+                    for m, half in ((tiles[0], 0), (tiles[0], 1), (tiles[1], 0))
+                ]
+                v_on_vector(tiles[1], 1, multiply(tiles[1], V, 1))
+                for value in values:
+                    v_on_gpsimd(*value)
+            else:
+                values = [(tiles[0], half, v_leaves_psum(multiply(tiles[0], V, half))) for half in range(HALVES)]
+                v_on_gpsimd(*values[0])
+                done = normalise_banks(waiting, done, done + 1)
+                v_on_vector(tiles[1], 0, multiply(tiles[1], V, 0))
+                v_on_gpsimd(*values[1])
+                done = normalise_banks(waiting, done, done + 1)
+                v_on_vector(tiles[1], 1, multiply(tiles[1], V, 1))

@@ -283,10 +283,8 @@ def tile_naswinattention_pa_kernel(
                 for value in values:
                     v_on_gpsimd(*value)
             else:
-                values = [(tiles[0], half, v_leaves_psum(multiply(tiles[0], V, half))) for half in range(HALVES)]
-                v_on_gpsimd(*values[0])
-                done = normalise_banks(waiting, done, done + 1)
-                v_on_vector(tiles[1], 0, multiply(tiles[1], V, 0))
-                v_on_gpsimd(*values[1])
-                done = normalise_banks(waiting, done, done + 1)
-                v_on_vector(tiles[1], 1, multiply(tiles[1], V, 1))
+                for half in range(HALVES):
+                    v_on_vector(tiles[0], half, multiply(tiles[0], V, half))
+                for half in range(HALVES):
+                    done = normalise_banks(waiting, done, done + 1)
+                    v_on_vector(tiles[1], half, multiply(tiles[1], V, half))

@@ -75,8 +75,8 @@ def tile_naswinattention_pa_kernel(
             nc.vector.memset(w_planes[s][:].bitcast(I32), 0)
 
         nc.gpsimd.memset(first_rows[:].bitcast(F32), 0.0)
-        make_identity(nc, ident[:])
         nc.gpsimd.memset(later_rows[:].bitcast(F32), 0.0)
+        make_identity(nc, ident[:])
         nc.vector.memset(eps[:], EPS)
         zero_planes(Q)
         nc.vector.memset(ones[:], 1.0)
@@ -86,9 +86,12 @@ def tile_naswinattention_pa_kernel(
         vid_by_window = vid.rearrange("(a n b) k -> n a b k", n=WINDOWS, b=WIN_W)
         runs = P // WIN_W
 
-        def load_tokens(m):
+        def load_tokens(m, pieces):
             n, c = divmod(m, TILES_PER_WINDOW)
-            nc.sync.dma_start(out=x_all[:, m, :], in_=vid_by_window[n, runs * c : runs * (c + 1)])
+            width = K // pieces
+            for i in range(pieces):
+                cols = slice(width * i, width * (i + 1))
+                nc.sync.dma_start(out=x_all[:, m, cols], in_=vid_by_window[n, runs * c : runs * (c + 1), :, cols])
 
         words_i32 = w_words.bitcast(I32)
         part_words = 2 * INNER // 4
@@ -111,24 +114,24 @@ def tile_naswinattention_pa_kernel(
                     ),
                 )
 
+        nc.scalar.activation(out=warm[:], in_=eps[:], func=ACT.Abs_reciprocal_sqrt)
         bias_row = bias.unsqueeze(0)
         nc.scalar.dma_start(out=first_rows[0:1, 0:INNER], in_=bias_row[:, 0:INNER])
         nc.scalar.dma_start(out=first_rows[0:1, INNER : INNER + HD], in_=q_gain.unsqueeze(0))
         nc.scalar.dma_start(out=first_rows[0:1, INNER + HD : INNER + 2 * HD], in_=k_gain.unsqueeze(0))
         nc.scalar.dma_start(out=later_rows[0:1, :], in_=bias_row[:, INNER : 3 * INNER])
-        nc.scalar.activation(out=warm[:], in_=eps[:], func=ACT.Abs_reciprocal_sqrt)
-        load_tokens(0)
-        load_tokens(1)
+        load_tokens(0, PASSES)
+        load_tokens(1, PASSES)
         load_scales(Q)
         load_words(Q)
-        load_tokens(2)
-        load_tokens(3)
+        load_tokens(2, 1)
+        load_tokens(3, 1)
         load_scales(KK)
         load_words(KK)
         load_scales(V)
         load_words(V)
         for m in range(4, TOKEN_TILES):
-            load_tokens(m)
+            load_tokens(m, 1)
 
         def transpose_units(first):
             xt = psum.tile([P, 2, 2, P], F32, tag="bank", name="xt")
@@ -253,6 +256,8 @@ def tile_naswinattention_pa_kernel(
             stop=True,
         )
         spread_bias(Q, nc.vector.tensor_copy)
+        spread_bias(KK, nc.vector.tensor_copy)
+        spread_bias(V, nc.scalar.copy)
 
         for j in range(BLOCKS):
             tiles = (PAIR * j, PAIR * j + 1)
@@ -264,9 +269,6 @@ def tile_naswinattention_pa_kernel(
                     done = normalise_banks(waiting, done, len(waiting))
                     banks = [transpose_units(UNITS * (j + 1) + 2 * c) for c in range(UNIT_BANKS)]
                     grouped = [group_units(xt) for xt in banks]
-                if s == KK and j == 0:
-                    spread_bias(KK, nc.vector.tensor_copy)
-                    spread_bias(V, nc.scalar.copy)
                 for i, (m, half) in enumerate([(m, half) for m in tiles for half in range(HALVES)]):
                     y = add_bias(multiply(m, s, half), s, half)
                     waiting.append((m, s, half, y, inverse_rms(y)))

@@ -51,6 +51,7 @@ def tile_naswinattention_pa_kernel(
         sums = ctx.enter_context(tc.tile_pool(name="sums", bufs=10))
         results = ctx.enter_context(tc.tile_pool(name="results", bufs=6))
         junk = ctx.enter_context(tc.tile_pool(name="junk", bufs=2))
+        slow = ctx.enter_context(tc.tile_pool(name="slow", bufs=4))
         psum = ctx.enter_context(tc.psum_pool(name="psum", bufs=7))
         psum_keep = ctx.enter_context(tc.psum_pool(name="psum_keep", bufs=1))
 
@@ -68,6 +69,7 @@ def tile_naswinattention_pa_kernel(
         warm = keep.tile([P, 1], F32)
         ident = keep.tile([P, P], F32)
         bias_bc = keep.tile([P, 3, INNER], BF16)
+        gain_rows = keep.tile([P, 2, BANK_HEADS, HD], F32)
         x_codes = keep.tile([P, TOKEN_TILES * PASSES, P], U32, align_bytes=64)
         x_planes = keep.tile([P, TOKEN_TILES * PASSES, P], U8, align_bytes=64)
 
@@ -225,6 +227,24 @@ def tile_naswinattention_pa_kernel(
                 )
             nc.sync.dma_start(out=out_rows(m, s, half), in_=normed[:])
 
+        def normalise_on_gpsimd(s, y, rstd):
+            normed = slow.tile([P, BANK_HEADS, HD], F32, name="normed_slow")
+            nc.gpsimd.tensor_tensor(
+                out=normed[:], in0=y[:].rearrange("p (h d) -> p h d", h=BANK_HEADS), in1=gain_rows[:, s], op=ALU.mult
+            )
+            nc.gpsimd.tensor_tensor(
+                out=normed[:],
+                in0=normed[:],
+                in1=rstd[:].unsqueeze(2).to_broadcast([P, BANK_HEADS, HD]),
+                op=ALU.mult,
+            )
+            return normed
+
+        def store_slow(late):
+            for m, s, half, normed in late:
+                nc.sync.dma_start(out=out_rows(m, s, half), in_=normed[:].rearrange("p h d -> p (h d)"))
+            late.clear()
+
         def normalise_banks(waiting, done, upto):
             for entry in waiting[done:upto]:
                 normalise_and_store(*entry)
@@ -258,25 +278,34 @@ def tile_naswinattention_pa_kernel(
         spread_bias(Q, nc.vector.tensor_copy)
         spread_bias(KK, nc.vector.tensor_copy)
         spread_bias(V, nc.scalar.copy)
+        for s in (Q, KK):
+            for h in range(BANK_HEADS):
+                nc.vector.tensor_copy(out=gain_rows[:, s, h, :], in_=gain_bc[:, s, :])
 
         for j in range(BLOCKS):
             tiles = (PAIR * j, PAIR * j + 1)
             last = j == BLOCKS - 1
             waiting = []
             done = 0
+            late = []
             for s in (Q, KK):
                 if s == KK and not last:
                     done = normalise_banks(waiting, done, len(waiting))
                     banks = [transpose_units(UNITS * (j + 1) + 2 * c) for c in range(UNIT_BANKS)]
                     grouped = [group_units(xt) for xt in banks]
+                store_slow(late)
                 for i, (m, half) in enumerate([(m, half) for m in tiles for half in range(HALVES)]):
                     y = add_bias(multiply(m, s, half), s, half)
-                    waiting.append((m, s, half, y, inverse_rms(y)))
+                    if i == 1:
+                        late.append((m, s, half, normalise_on_gpsimd(s, y, inverse_rms(y))))
+                    else:
+                        waiting.append((m, s, half, y, inverse_rms(y)))
                     done = normalise_banks(waiting, done, len(waiting) - LAG)
                     if s == KK and not last and i < UNIT_BANKS:
                         quantise_units(UNITS * (j + 1) + 2 * i, grouped[i])
             if not last:
                 done = normalise_banks(waiting, done, len(waiting))
+                store_slow(late)
                 values = [
                     (m, half, v_leaves_psum(multiply(m, V, half)))
                     for m, half in ((tiles[0], 0), (tiles[0], 1), (tiles[1], 0))
@@ -285,6 +314,7 @@ def tile_naswinattention_pa_kernel(
                 for value in values:
                     v_on_gpsimd(*value)
             else:
+                store_slow(late)
                 for half in range(HALVES):
                     v_on_vector(tiles[0], half, multiply(tiles[0], V, half))
                 for half in range(HALVES):

@@ -199,19 +199,20 @@ def tile_naswinattention_pa_kernel(
             nc.vector.tensor_tensor(out=y[:], in0=acc[:], in1=bias_of(s, half), op=ALU.add)
             return y
 
-        def inverse_rms(y):
+        def sum_squares(y, sumsq):
             squares = junk.tile([P, BANK], BF16, name="squares")
-            sumsq = sums.tile([P, BANK_HEADS], F32, name="sumsq")
             for h in range(BANK_HEADS):
                 head = slice(HD * h, HD * (h + 1))
                 nc.scalar.activation(
                     out=squares[:, head], in_=y[:, head], func=ACT.Square, accum_out=sumsq[:, h : h + 1]
                 )
-            rstd = sums.tile([P, BANK_HEADS], F32, name="rstd")
-            nc.scalar.activation(
-                out=rstd[:], in_=sumsq[:], func=ACT.Abs_reciprocal_sqrt, bias=eps[:, 0:1], scale=1.0 / HD
-            )
-            return rstd
+
+        def inverse_rms(due):
+            for sumsq, rstd in due:
+                nc.scalar.activation(
+                    out=rstd[:], in_=sumsq[:], func=ACT.Abs_reciprocal_sqrt, bias=eps[:, 0:1], scale=1.0 / HD
+                )
+            due.clear()
 
         def normalise_and_store(m, s, half, y, rstd):
             normed = results.tile([P, BANK], F32, name="normed")
@@ -227,18 +228,21 @@ def tile_naswinattention_pa_kernel(
                 )
             nc.sync.dma_start(out=out_rows(m, s, half), in_=normed[:])
 
-        def normalise_on_gpsimd(s, y, rstd):
+        def gain_on_gpsimd(s, y):
             normed = slow.tile([P, BANK_HEADS, HD], F32, name="normed_slow")
             nc.gpsimd.tensor_tensor(
                 out=normed[:], in0=y[:].rearrange("p (h d) -> p h d", h=BANK_HEADS), in1=gain_rows[:, s], op=ALU.mult
             )
+            return normed
+
+        def rms_on_gpsimd(m, s, half, y, rstd, normed):
             nc.gpsimd.tensor_tensor(
                 out=normed[:],
                 in0=normed[:],
                 in1=rstd[:].unsqueeze(2).to_broadcast([P, BANK_HEADS, HD]),
                 op=ALU.mult,
             )
-            return normed
+            return (m, s, half, normed)
 
         def store_slow(late):
             for m, s, half, normed in late:
@@ -288,28 +292,40 @@ def tile_naswinattention_pa_kernel(
             waiting = []
             done = 0
             late = []
+            due = []
             for s in (Q, KK):
                 if s == KK and not last:
-                    done = normalise_banks(waiting, done, len(waiting))
                     banks = [transpose_units(UNITS * (j + 1) + 2 * c) for c in range(UNIT_BANKS)]
-                    grouped = [group_units(xt) for xt in banks]
+                    grouped = [group_units(banks[0])]
+                    inverse_rms(due)
+                    grouped += [group_units(xt) for xt in banks[1:]]
+                    done = normalise_banks(waiting, done, len(waiting))
                 store_slow(late)
                 for i, (m, half) in enumerate([(m, half) for m in tiles for half in range(HALVES)]):
                     y = add_bias(multiply(m, s, half), s, half)
+                    sumsq = sums.tile([P, BANK_HEADS], F32, name="sumsq")
+                    rstd = sums.tile([P, BANK_HEADS], F32, name="rstd")
+                    sum_squares(y, sumsq)
+                    inverse_rms(due)
+                    due.append((sumsq, rstd))
                     if i == 1:
-                        late.append((m, s, half, normalise_on_gpsimd(s, y, inverse_rms(y))))
+                        slow_bank = (m, s, half, y, rstd, gain_on_gpsimd(s, y))
                     else:
-                        waiting.append((m, s, half, y, inverse_rms(y)))
+                        waiting.append((m, s, half, y, rstd))
+                    if i == 2:
+                        late.append(rms_on_gpsimd(*slow_bank))
+                    if s == KK and i == 3 and last:
+                        inverse_rms(due)
                     done = normalise_banks(waiting, done, len(waiting) - LAG)
                     if s == KK and not last and i < UNIT_BANKS:
                         quantise_units(UNITS * (j + 1) + 2 * i, grouped[i])
             if not last:
-                done = normalise_banks(waiting, done, len(waiting))
                 store_slow(late)
-                values = [
-                    (m, half, v_leaves_psum(multiply(m, V, half)))
-                    for m, half in ((tiles[0], 0), (tiles[0], 1), (tiles[1], 0))
-                ]
+                values = []
+                for m, half in ((tiles[0], 0), (tiles[0], 1), (tiles[1], 0)):
+                    values.append((m, half, v_leaves_psum(multiply(m, V, half))))
+                    inverse_rms(due)
+                done = normalise_banks(waiting, done, len(waiting))
                 v_on_vector(tiles[1], 1, multiply(tiles[1], V, 1))
                 for value in values:
                     v_on_gpsimd(*value)

@@ -107,13 +107,12 @@ def tile_naswinattention_pa_kernel(
         scales_i32 = w_scales.bitcast(I32)
         part_i32 = INNER // 4
 
+        scale_rows = scales_i32.rearrange("g (quad r) c -> r quad g c", r=4)
+
         def load_scales(s):
-            for quad in range(4):
+            for r in range(4):
                 nc.sync.dma_start(
-                    out=w_planes[s][32 * quad : 32 * quad + 4].bitcast(I32),
-                    in_=scales_i32[:, 4 * quad : 4 * quad + 4, part_i32 * s : part_i32 * (s + 1)].rearrange(
-                        "g r c -> r g c"
-                    ),
+                    out=w_planes[s][r:P:32].bitcast(I32), in_=scale_rows[r, :, :, part_i32 * s : part_i32 * (s + 1)]
                 )
 
         nc.scalar.activation(out=warm[:], in_=eps[:], func=ACT.Abs_reciprocal_sqrt)

@@ -34,6 +34,20 @@ PAIR = 2
 BLOCKS = TOKEN_TILES // PAIR
 UNITS = PAIR * PASSES
 UNIT_BANKS = UNITS // 2
+STEPS = [("Q", 0), ("T", 1), ("K", 0), ("V", 0), ("Q", 1), ("T", 2), ("K", 1), ("V", 1), ("Q", 2), ("T", 3), ("K", 2), ("V", 2), ("Q", 3), ("L", 3)]
+TAIL = "s k00 k01 v00 k10 v01 k11 v10 r s n n v11".split(" ")
+
+
+def SLOW(m, s, half):
+    return m % 2 == 0 and half == 1
+
+
+def VSL(j, i):
+    return i < 3
+
+
+VF = 2
+MIDH = 1
 LAG = 2
 
 FLOPS = 2 * L_VID * K * 3 * INNER
@@ -198,13 +212,15 @@ def tile_naswinattention_pa_kernel(
             nc.vector.tensor_tensor(out=y[:], in0=acc[:], in1=bias_of(s, half), op=ALU.add)
             return y
 
-        def sum_squares(y, sumsq):
+        def sum_squares(y, sumsq, due):
             squares = junk.tile([P, BANK], BF16, name="squares")
             for h in range(BANK_HEADS):
                 head = slice(HD * h, HD * (h + 1))
                 nc.scalar.activation(
                     out=squares[:, head], in_=y[:, head], func=ACT.Square, accum_out=sumsq[:, h : h + 1]
                 )
+                if h == MIDH:
+                    inverse_rms(due)
 
         def inverse_rms(due):
             for sumsq, rstd in due:
@@ -285,53 +301,100 @@ def tile_naswinattention_pa_kernel(
             for h in range(BANK_HEADS):
                 nc.vector.tensor_copy(out=gain_rows[:, s, h, :], in_=gain_bc[:, s, :])
 
-        for j in range(BLOCKS):
-            tiles = (PAIR * j, PAIR * j + 1)
-            last = j == BLOCKS - 1
-            waiting = []
-            done = 0
-            late = []
-            due = []
-            for s in (Q, KK):
-                if s == KK and not last:
-                    banks = [transpose_units(UNITS * (j + 1) + 2 * c) for c in range(UNIT_BANKS)]
-                    grouped = [group_units(banks[0])]
-                    inverse_rms(due)
-                    grouped += [group_units(xt) for xt in banks[1:]]
-                    done = normalise_banks(waiting, done, len(waiting))
-                store_slow(late)
-                for i, (m, half) in enumerate([(m, half) for m in tiles for half in range(HALVES)]):
-                    y = add_bias(multiply(m, s, half), s, half)
+        waiting = []
+        due = []
+        late = []
+        fresh = []
+        slow_bank = []
+
+        def normalise_waiting(keep_back):
+            while len(waiting) > keep_back:
+                normalise_and_store(*waiting.pop(0))
+
+        def heavy_banks(s, tiles):
+            for m in tiles:
+                for half in range(HALVES):
+                    heavy_bank(m, s, half)
+
+        def heavy_bank(m, s, half):
+            if True:
+                if True:
+                    acc = multiply(m, s, half)
+                    y = add_bias(acc, s, half)
+                    if fresh:
+                        quantise_units(*fresh.pop(0))
                     sumsq = sums.tile([P, BANK_HEADS], F32, name="sumsq")
                     rstd = sums.tile([P, BANK_HEADS], F32, name="rstd")
-                    sum_squares(y, sumsq)
-                    inverse_rms(due)
+                    sum_squares(y, sumsq, due)
                     due.append((sumsq, rstd))
-                    if i == 1:
-                        slow_bank = (m, s, half, y, rstd, gain_on_gpsimd(s, y))
+                    while slow_bank:
+                        late.append(rms_on_gpsimd(*slow_bank.pop()))
+                    if SLOW(m, s, half):
+                        slow_bank.append((m, s, half, y, rstd, gain_on_gpsimd(s, y)))
                     else:
                         waiting.append((m, s, half, y, rstd))
-                    if i == 2:
-                        late.append(rms_on_gpsimd(*slow_bank))
-                    if s == KK and i == 3 and last:
-                        inverse_rms(due)
-                    done = normalise_banks(waiting, done, len(waiting) - LAG)
-                    if s == KK and not last and i < UNIT_BANKS:
-                        quantise_units(UNITS * (j + 1) + 2 * i, grouped[i])
-            if not last:
+                    normalise_waiting(LAG)
+
+        def light_on_scalar(m, half):
+            value = v_leaves_psum(multiply(m, V, half))
+            inverse_rms(due)
+            return (m, half, value)
+
+        for step in STEPS:
+            kind, j = step
+            tiles = (PAIR * j, PAIR * j + 1)
+            if kind == "B":
+                spread_bias(KK, nc.vector.tensor_copy)
+                spread_bias(V, nc.scalar.copy)
+            elif kind == "T":
+                first = UNITS * j
+                banks = [transpose_units(first + 2 * c) for c in range(UNIT_BANKS)]
+                for c, xt in enumerate(banks):
+                    fresh.append((first + 2 * c, group_units(xt)))
+                    inverse_rms(due)
+                normalise_waiting(1)
+                quantise_units(*fresh.pop(0))
+                normalise_waiting(0)
+            elif kind == "q":
+                store_slow(late)
+                heavy_banks(Q, (j,))
+            elif kind == "Q":
+                store_slow(late)
+                heavy_banks(Q, tiles)
+            elif kind == "K":
+                store_slow(late)
+                heavy_banks(KK, tiles)
+            elif kind == "V" and j < BLOCKS - 1:
                 store_slow(late)
                 values = []
-                for m, half in ((tiles[0], 0), (tiles[0], 1), (tiles[1], 0)):
-                    values.append((m, half, v_leaves_psum(multiply(m, V, half))))
-                    inverse_rms(due)
-                done = normalise_banks(waiting, done, len(waiting))
-                v_on_vector(tiles[1], 1, multiply(tiles[1], V, 1))
+                for i, (m, half) in enumerate([(m, half) for m in tiles for half in range(HALVES)]):
+                    if VSL(j, i):
+                        values.append(light_on_scalar(m, half))
+                        if i == VF:
+                            normalise_waiting(0)
+                    else:
+                        if i <= VF:
+                            normalise_waiting(0)
+                        v_on_vector(m, half, multiply(m, V, half))
                 for value in values:
                     v_on_gpsimd(*value)
             else:
-                store_slow(late)
-                for half in range(HALVES):
-                    v_on_vector(tiles[0], half, multiply(tiles[0], V, half))
-                for half in range(HALVES):
-                    done = normalise_banks(waiting, done, done + 1)
-                    v_on_vector(tiles[1], half, multiply(tiles[1], V, half))
+                for item in TAIL:
+                    if item == "n":
+                        normalise_waiting(max(0, len(waiting) - 1))
+                    elif item == "s":
+                        store_slow(late)
+                    elif item == "r":
+                        inverse_rms(due)
+                    elif item[0] == "k":
+                        m, half = tiles[int(item[1])], int(item[2])
+                        heavy_bank(m, KK, half)
+                    elif item[0] == "v":
+                        m, half = tiles[int(item[1])], int(item[2])
+                        v_on_vector(m, half, multiply(m, V, half))
+                    elif item[0] == "w":
+                        m, half = tiles[int(item[1])], int(item[2])
+                        slowv = light_on_scalar(m, half)
+                        nc.gpsimd.tensor_tensor(out=slowv[2][:], in0=slowv[2][:], in1=bias_of(V, half), op=ALU.add)
+                    elif item[0] == "x":
+                        nc.sync.dma_start(out=out_rows(slowv[0], V, slowv[1]), in_=slowv[2][:])

@@ -43,7 +43,7 @@ def SLOW(m, s, half):
 
 
 def VSL(j, i):
-    return i < 3
+    return j < 2 or i < 3
 
 
 VF = 2
@@ -87,17 +87,17 @@ def tile_naswinattention_pa_kernel(
         x_codes = keep.tile([P, TOKEN_TILES * PASSES, P], U32, align_bytes=64)
         x_planes = keep.tile([P, TOKEN_TILES * PASSES, P], U8, align_bytes=64)
 
-        def zero_planes(s):
-            nc.vector.memset(w_planes[s][:].bitcast(I32), 0)
+        def zero_planes(s, engine):
+            engine.memset(w_planes[s][:].bitcast(I32), 0)
 
         nc.gpsimd.memset(first_rows[:].bitcast(F32), 0.0)
         nc.gpsimd.memset(later_rows[:].bitcast(F32), 0.0)
         make_identity(nc, ident[:])
         nc.vector.memset(eps[:], EPS)
-        zero_planes(Q)
+        zero_planes(Q, nc.vector)
         nc.vector.memset(ones[:], 1.0)
-        zero_planes(KK)
-        zero_planes(V)
+        zero_planes(KK, nc.gpsimd)
+        zero_planes(V, nc.gpsimd)
 
         vid_by_window = vid.rearrange("(a n b) k -> n a b k", n=WINDOWS, b=WIN_W)
         runs = P // WIN_W
@@ -295,11 +295,11 @@ def tile_naswinattention_pa_kernel(
             stop=True,
         )
         spread_bias(Q, nc.vector.tensor_copy)
-        spread_bias(KK, nc.vector.tensor_copy)
+        spread_bias(KK, nc.scalar.copy)
         spread_bias(V, nc.scalar.copy)
         for s in (Q, KK):
             for h in range(BANK_HEADS):
-                nc.vector.tensor_copy(out=gain_rows[:, s, h, :], in_=gain_bc[:, s, :])
+                nc.scalar.copy(out=gain_rows[:, s, h, :], in_=gain_bc[:, s, :])
 
         waiting = []
         due = []

@@ -35,11 +35,11 @@ BLOCKS = TOKEN_TILES // PAIR
 UNITS = PAIR * PASSES
 UNIT_BANKS = UNITS // 2
 STEPS = [("Q", 0), ("T", 1), ("K", 0), ("V", 0), ("Q", 1), ("T", 2), ("K", 1), ("V", 1), ("Q", 2), ("T", 3), ("K", 2), ("V", 2), ("Q", 3), ("L", 3)]
-TAIL = "s k00 k01 v00 k10 v01 k11 v10 r s n n v11".split(" ")
+TAIL = "k00 k01 v00 s k10 v01 k11 v10 r s n n v11".split(" ")
 
 
 def SLOW(m, s, half):
-    return m % 2 == 0 and half == 1
+    return m % 2 == 0 and half == 1 and not (m == 6 and s == KK)
 
 
 def VSL(j, i):
@@ -48,6 +48,7 @@ def VSL(j, i):
 
 VF = 2
 MIDH = 1
+GD = 4
 LAG = 2
 
 FLOPS = 2 * L_VID * K * 3 * INNER
@@ -62,10 +63,10 @@ def tile_naswinattention_pa_kernel(
         ctx.enter_context(tc.manual_schedule())
         keep = ctx.enter_context(tc.tile_pool(name="keep", bufs=1))
         stage = ctx.enter_context(tc.tile_pool(name="stage", bufs=4))
-        sums = ctx.enter_context(tc.tile_pool(name="sums", bufs=10))
-        results = ctx.enter_context(tc.tile_pool(name="results", bufs=6))
+        sums = ctx.enter_context(tc.tile_pool(name="sums", bufs=14))
+        results = ctx.enter_context(tc.tile_pool(name="results", bufs=10))
         junk = ctx.enter_context(tc.tile_pool(name="junk", bufs=2))
-        slow = ctx.enter_context(tc.tile_pool(name="slow", bufs=4))
+        slow = ctx.enter_context(tc.tile_pool(name="slow", bufs=6))
         psum = ctx.enter_context(tc.psum_pool(name="psum", bufs=7))
         psum_keep = ctx.enter_context(tc.psum_pool(name="psum_keep", bufs=1))
 
@@ -304,8 +305,16 @@ def tile_naswinattention_pa_kernel(
         waiting = []
         due = []
         late = []
+        clock = [0]
+        late_v = []
+        heavy_count = [0]
         fresh = []
         slow_bank = []
+
+        def release(age):
+            while late and clock[0] - late[0][4] >= age:
+                m, s, half, normed = late.pop(0)[:4]
+                nc.sync.dma_start(out=out_rows(m, s, half), in_=normed[:].rearrange("p h d -> p (h d)"))
 
         def normalise_waiting(keep_back):
             while len(waiting) > keep_back:
@@ -328,12 +337,18 @@ def tile_naswinattention_pa_kernel(
                     sum_squares(y, sumsq, due)
                     due.append((sumsq, rstd))
                     while slow_bank:
-                        late.append(rms_on_gpsimd(*slow_bank.pop()))
+                        late.append(rms_on_gpsimd(*slow_bank.pop()) + (clock[0],))
                     if SLOW(m, s, half):
                         slow_bank.append((m, s, half, y, rstd, gain_on_gpsimd(s, y)))
                     else:
                         waiting.append((m, s, half, y, rstd))
                     normalise_waiting(LAG)
+                    if late_v and heavy_count[0] % 4 >= 1:
+                        mm, hh, value = late_v.pop(0)
+                        nc.sync.dma_start(out=out_rows(mm, V, hh), in_=value[:])
+                    heavy_count[0] += 1
+                    clock[0] += 1
+                    release(GD)
 
         def light_on_scalar(m, half):
             value = v_leaves_psum(multiply(m, V, half))
@@ -356,16 +371,16 @@ def tile_naswinattention_pa_kernel(
                 quantise_units(*fresh.pop(0))
                 normalise_waiting(0)
             elif kind == "q":
-                store_slow(late)
+                release(GD)
                 heavy_banks(Q, (j,))
             elif kind == "Q":
-                store_slow(late)
+                release(GD)
                 heavy_banks(Q, tiles)
             elif kind == "K":
-                store_slow(late)
+                release(GD)
                 heavy_banks(KK, tiles)
             elif kind == "V" and j < BLOCKS - 1:
-                store_slow(late)
+                release(GD)
                 values = []
                 for i, (m, half) in enumerate([(m, half) for m in tiles for half in range(HALVES)]):
                     if VSL(j, i):
@@ -376,14 +391,17 @@ def tile_naswinattention_pa_kernel(
                         if i <= VF:
                             normalise_waiting(0)
                         v_on_vector(m, half, multiply(m, V, half))
-                for value in values:
-                    v_on_gpsimd(*value)
+                clock[0] += 3
+                release(GD)
+                for m, half, value in values:
+                    nc.gpsimd.tensor_tensor(out=value[:], in0=value[:], in1=bias_of(V, half), op=ALU.add)
+                late_v.extend(values)
             else:
                 for item in TAIL:
                     if item == "n":
                         normalise_waiting(max(0, len(waiting) - 1))
                     elif item == "s":
-                        store_slow(late)
+                        release(0)
                     elif item == "r":
                         inverse_rms(due)
                     elif item[0] == "k":

from contextlib import ExitStack

import concourse.mybir as mybir
from concourse.masks import make_identity

F32 = mybir.dt.float32
BF16 = mybir.dt.bfloat16
I32 = mybir.dt.int32
U32 = mybir.dt.uint32
U8 = mybir.dt.uint8
FP8X4 = mybir.dt.float8_e4m3fn_x4
FP4X4 = mybir.dt.float4_e2m1fn_x4
ALU = mybir.AluOpType
ACT = mybir.ActivationFunctionType

P = 128
L_VID = 1024
K = 1536
K_PASS = 512
PASSES = K // K_PASS
HEADS = 8
HD = 128
INNER = HEADS * HD
BANK = 512
HALVES = INNER // BANK
BANK_HEADS = BANK // HD
TOKEN_TILES = L_VID // P
WINDOWS = 2
TILES_PER_WINDOW = TOKEN_TILES // WINDOWS
WIN_W = 8
EPS = 1e-6
Q, KK, V = 0, 1, 2
PAIR = 2
BLOCKS = TOKEN_TILES // PAIR
UNITS = PAIR * PASSES
UNIT_BANKS = UNITS // 2
STEPS = [("Q", 0), ("T", 1), ("K", 0), ("V", 0), ("Q", 1), ("T", 2), ("K", 1), ("V", 1), ("Q", 2), ("T", 3), ("K", 2), ("V", 2), ("Q", 3), ("L", 3)]
TAIL = "k00 k01 v00 s k10 v01 k11 v10 r s n n v11".split(" ")


def SLOW(m, s, half):
    return m % 2 == 0 and half == 1 and not (m == 6 and s == KK)


def VSL(j, i):
    return j < 2 or i < 3


VF = 2
MIDH = 1
GD = 4
LAG = 2

FLOPS = 2 * L_VID * K * 3 * INNER


def tile_naswinattention_pa_kernel(
    tc, vid, w_words, w_scales, bias, q_gain, k_gain, out_q, out_k, out_v
):
    nc = tc.nc
    outs = (out_q, out_k, out_v)
    with ExitStack() as ctx:
        ctx.enter_context(tc.manual_schedule())
        keep = ctx.enter_context(tc.tile_pool(name="keep", bufs=1))
        stage = ctx.enter_context(tc.tile_pool(name="stage", bufs=4))
        sums = ctx.enter_context(tc.tile_pool(name="sums", bufs=14))
        results = ctx.enter_context(tc.tile_pool(name="results", bufs=10))
        junk = ctx.enter_context(tc.tile_pool(name="junk", bufs=2))
        slow = ctx.enter_context(tc.tile_pool(name="slow", bufs=6))
        psum = ctx.enter_context(tc.psum_pool(name="psum", bufs=7))
        psum_keep = ctx.enter_context(tc.psum_pool(name="psum_keep", bufs=1))

        x_all = keep.tile([P, TOKEN_TILES, K], BF16)
        w_codes = {
            Q: [keep.tile([P, PASSES, 2 * BANK], U8, align_bytes=64, name="codes_q%d" % half) for half in range(HALVES)],
            KK: [keep.tile([P, PASSES, 2 * INNER], U8, align_bytes=64, name="codes_k")],
            V: [keep.tile([P, PASSES, 2 * INNER], U8, align_bytes=64, name="codes_v")],
        }
        w_planes = [keep.tile([P, PASSES, INNER], U8, align_bytes=64, name="planes%d" % s) for s in (Q, KK, V)]
        first_rows = keep.tile([P, INNER + 2 * HD], BF16)
        later_rows = keep.tile([P, 2 * INNER], BF16)
        ones = keep.tile([P, P], BF16)
        eps = keep.tile([P, 1], F32)
        warm = keep.tile([P, 1], F32)
        ident = keep.tile([P, P], F32)
        bias_bc = keep.tile([P, 3, INNER], BF16)
        gain_rows = keep.tile([P, 2, BANK_HEADS, HD], F32)
        x_codes = keep.tile([P, TOKEN_TILES * PASSES, P], U32, align_bytes=64)
        x_planes = keep.tile([P, TOKEN_TILES * PASSES, P], U8, align_bytes=64)

        def zero_planes(s, engine):
            engine.memset(w_planes[s][:].bitcast(I32), 0)

        nc.gpsimd.memset(first_rows[:].bitcast(F32), 0.0)
        nc.gpsimd.memset(later_rows[:].bitcast(F32), 0.0)
        make_identity(nc, ident[:])
        nc.vector.memset(eps[:], EPS)
        zero_planes(Q, nc.vector)
        nc.vector.memset(ones[:], 1.0)
        zero_planes(KK, nc.gpsimd)
        zero_planes(V, nc.gpsimd)

        vid_by_window = vid.rearrange("(a n b) k -> n a b k", n=WINDOWS, b=WIN_W)
        runs = P // WIN_W

        def load_tokens(m, pieces):
            n, c = divmod(m, TILES_PER_WINDOW)
            width = K // pieces
            for i in range(pieces):
                cols = slice(width * i, width * (i + 1))
                nc.sync.dma_start(out=x_all[:, m, cols], in_=vid_by_window[n, runs * c : runs * (c + 1), :, cols])

        words_i32 = w_words.bitcast(I32)
        part_words = 2 * INNER // 4

        def load_words(s):
            width = part_words // len(w_codes[s])
            for i, codes in enumerate(w_codes[s]):
                cols = slice(part_words * s + width * i, part_words * s + width * (i + 1))
                nc.sync.dma_start(out=codes[:].bitcast(I32), in_=words_i32[:, :, cols].rearrange("g p c -> p g c"))

        scales_i32 = w_scales.bitcast(I32)
        part_i32 = INNER // 4

        scale_rows = scales_i32.rearrange("g (quad r) c -> r quad g c", r=4)

        def load_scales(s):
            for r in range(4):
                nc.sync.dma_start(
                    out=w_planes[s][r:P:32].bitcast(I32), in_=scale_rows[r, :, :, part_i32 * s : part_i32 * (s + 1)]
                )

        nc.scalar.activation(out=warm[:], in_=eps[:], func=ACT.Abs_reciprocal_sqrt)
        bias_row = bias.unsqueeze(0)
        nc.scalar.dma_start(out=first_rows[0:1, 0:INNER], in_=bias_row[:, 0:INNER])
        nc.scalar.dma_start(out=first_rows[0:1, INNER : INNER + HD], in_=q_gain.unsqueeze(0))
        nc.scalar.dma_start(out=first_rows[0:1, INNER + HD : INNER + 2 * HD], in_=k_gain.unsqueeze(0))
        nc.scalar.dma_start(out=later_rows[0:1, :], in_=bias_row[:, INNER : 3 * INNER])
        load_tokens(0, PASSES)
        load_tokens(1, PASSES)
        load_scales(Q)
        load_words(Q)
        load_tokens(2, 1)
        load_tokens(3, 1)
        load_scales(KK)
        load_words(KK)
        load_scales(V)
        load_words(V)
        for m in range(4, TOKEN_TILES):
            load_tokens(m, 1)

        def transpose_units(first):
            xt = psum.tile([P, 2, 2, P], F32, tag="bank", name="xt")
            for i in range(2):
                m, g = divmod(first + i, PASSES)
                words = x_all[:, m, :].bitcast(F32)
                for u in range(2):
                    nc.tensor.transpose(xt[:, i, u, :], words[:, 256 * g + u : 256 * (g + 1) : 2], ident[:])
            return xt

        def group_units(xt):
            grouped = stage.tile([P, 2, P, 4], BF16, align_bytes=64, name="grouped")
            nc.scalar.copy(out=grouped[:].bitcast(F32), in_=xt[:].rearrange("p i u r -> p i r u"))
            return grouped

        def quantise_units(first, grouped):
            nc.vector.quantize_mx(
                out=x_codes[:, first : first + 2, :].rearrange("p i r -> p (i r)").bitcast(FP8X4),
                scales=x_planes[:, first : first + 2, :].rearrange("p i r -> p (i r)"),
                in_=grouped[:].rearrange("p i r t -> p (i r t)"),
            )

        def spread_bias(s, engine_copy):
            spread = psum.tile([P, INNER], BF16, tag="bank", name="spread")
            for half in range(HALVES):
                cols = slice(BANK * half, BANK * (half + 1))
                nc.tensor.matmul(
                    out=spread[:, cols],
                    lhsT=ones[:],
                    rhs=(first_rows if s == Q else later_rows)[:, INNER * max(s - 1, 0) + BANK * half :][:, 0:BANK],
                    start=True,
                    stop=True,
                )
            engine_copy(out=bias_bc[:, s, :], in_=spread[:])

        def out_rows(m, s, half):
            n, c = divmod(m, TILES_PER_WINDOW)
            return outs[s][n, P * c : P * (c + 1)].rearrange("p h d -> p (h d)")[:, BANK * half : BANK * (half + 1)]

        def multiply(m, s, half):
            col0 = BANK * half
            tiles_of_part = len(w_codes[s])
            codes = w_codes[s][half * tiles_of_part // HALVES]
            code0 = 2 * col0 % (2 * INNER // tiles_of_part)
            acc = psum.tile([P, BANK], F32, tag="bank", name="acc")
            for g in range(PASSES):
                nc.tensor.matmul_mx(
                    out=acc[:],
                    lhsT=x_codes[:, PASSES * m + g, :].bitcast(FP8X4),
                    lhsT_scale=x_planes[:, PASSES * m + g, :],
                    rhs=codes[:, g, code0 : code0 + 2 * BANK].bitcast(FP4X4),
                    rhs_scale=w_planes[s][:, g, col0 : col0 + BANK],
                    start=(g == 0),
                    stop=(g == PASSES - 1),
                )
            return acc

        def bias_of(s, half):
            return bias_bc[:, s, BANK * half : BANK * (half + 1)]

        def add_bias(acc, s, half):
            y = sums.tile([P, BANK], F32, name="y")
            nc.vector.tensor_tensor(out=y[:], in0=acc[:], in1=bias_of(s, half), op=ALU.add)
            return y

        def sum_squares(y, sumsq, due):
            squares = junk.tile([P, BANK], BF16, name="squares")
            for h in range(BANK_HEADS):
                head = slice(HD * h, HD * (h + 1))
                nc.scalar.activation(
                    out=squares[:, head], in_=y[:, head], func=ACT.Square, accum_out=sumsq[:, h : h + 1]
                )
                if h == MIDH:
                    inverse_rms(due)

        def inverse_rms(due):
            for sumsq, rstd in due:
                nc.scalar.activation(
                    out=rstd[:], in_=sumsq[:], func=ACT.Abs_reciprocal_sqrt, bias=eps[:, 0:1], scale=1.0 / HD
                )
            due.clear()

        def normalise_and_store(m, s, half, y, rstd):
            normed = results.tile([P, BANK], F32, name="normed")
            for h in range(BANK_HEADS):
                head = slice(HD * h, HD * (h + 1))
                nc.vector.scalar_tensor_tensor(
                    out=normed[:, head],
                    in0=y[:, head],
                    scalar=rstd[:, h : h + 1],
                    in1=gain_bc[:, s, :],
                    op0=ALU.mult,
                    op1=ALU.mult,
                )
            nc.sync.dma_start(out=out_rows(m, s, half), in_=normed[:])

        def gain_on_gpsimd(s, y):
            normed = slow.tile([P, BANK_HEADS, HD], F32, name="normed_slow")
            nc.gpsimd.tensor_tensor(
                out=normed[:], in0=y[:].rearrange("p (h d) -> p h d", h=BANK_HEADS), in1=gain_rows[:, s], op=ALU.mult
            )
            return normed

        def rms_on_gpsimd(m, s, half, y, rstd, normed):
            nc.gpsimd.tensor_tensor(
                out=normed[:],
                in0=normed[:],
                in1=rstd[:].unsqueeze(2).to_broadcast([P, BANK_HEADS, HD]),
                op=ALU.mult,
            )
            return (m, s, half, normed)

        def store_slow(late):
            for m, s, half, normed in late:
                nc.sync.dma_start(out=out_rows(m, s, half), in_=normed[:].rearrange("p h d -> p (h d)"))
            late.clear()

        def normalise_banks(waiting, done, upto):
            for entry in waiting[done:upto]:
                normalise_and_store(*entry)
            return max(done, upto)

        def v_on_vector(m, half, acc):
            value = results.tile([P, BANK], F32, name="value")
            nc.vector.tensor_tensor(out=value[:], in0=acc[:], in1=bias_of(V, half), op=ALU.add)
            nc.sync.dma_start(out=out_rows(m, V, half), in_=value[:])

        def v_leaves_psum(acc):
            value = results.tile([P, BANK], F32, name="value")
            nc.scalar.copy(out=value[:], in_=acc[:])
            return value

        def v_on_gpsimd(m, half, value):
            nc.gpsimd.tensor_tensor(out=value[:], in0=value[:], in1=bias_of(V, half), op=ALU.add)
            nc.sync.dma_start(out=out_rows(m, V, half), in_=value[:])

        banks = [transpose_units(2 * c) for c in range(UNIT_BANKS)]
        for c in range(UNIT_BANKS):
            quantise_units(2 * c, group_units(banks[c]))
        gain_bc = psum_keep.tile([P, 2, HD], F32)
        nc.tensor.matmul(
            out=gain_bc[:].rearrange("p s d -> p (s d)"),
            lhsT=ones[:],
            rhs=first_rows[:, INNER : INNER + 2 * HD],
            start=True,
            stop=True,
        )
        spread_bias(Q, nc.vector.tensor_copy)
        spread_bias(KK, nc.scalar.copy)
        spread_bias(V, nc.scalar.copy)
        for s in (Q, KK):
            for h in range(BANK_HEADS):
                nc.scalar.copy(out=gain_rows[:, s, h, :], in_=gain_bc[:, s, :])

        waiting = []
        due = []
        late = []
        clock = [0]
        late_v = []
        heavy_count = [0]
        fresh = []
        slow_bank = []

        def release(age):
            while late and clock[0] - late[0][4] >= age:
                m, s, half, normed = late.pop(0)[:4]
                nc.sync.dma_start(out=out_rows(m, s, half), in_=normed[:].rearrange("p h d -> p (h d)"))

        def normalise_waiting(keep_back):
            while len(waiting) > keep_back:
                normalise_and_store(*waiting.pop(0))

        def heavy_banks(s, tiles):
            for m in tiles:
                for half in range(HALVES):
                    heavy_bank(m, s, half)

        def heavy_bank(m, s, half):
            if True:
                if True:
                    acc = multiply(m, s, half)
                    y = add_bias(acc, s, half)
                    if fresh:
                        quantise_units(*fresh.pop(0))
                    sumsq = sums.tile([P, BANK_HEADS], F32, name="sumsq")
                    rstd = sums.tile([P, BANK_HEADS], F32, name="rstd")
                    sum_squares(y, sumsq, due)
                    due.append((sumsq, rstd))
                    while slow_bank:
                        late.append(rms_on_gpsimd(*slow_bank.pop()) + (clock[0],))
                    if SLOW(m, s, half):
                        slow_bank.append((m, s, half, y, rstd, gain_on_gpsimd(s, y)))
                    else:
                        waiting.append((m, s, half, y, rstd))
                    normalise_waiting(LAG)
                    if late_v and heavy_count[0] % 4 >= 1:
                        mm, hh, value = late_v.pop(0)
                        nc.sync.dma_start(out=out_rows(mm, V, hh), in_=value[:])
                    heavy_count[0] += 1
                    clock[0] += 1
                    release(GD)

        def light_on_scalar(m, half):
            value = v_leaves_psum(multiply(m, V, half))
            inverse_rms(due)
            return (m, half, value)

        for step in STEPS:
            kind, j = step
            tiles = (PAIR * j, PAIR * j + 1)
            if kind == "B":
                spread_bias(KK, nc.vector.tensor_copy)
                spread_bias(V, nc.scalar.copy)
            elif kind == "T":
                first = UNITS * j
                banks = [transpose_units(first + 2 * c) for c in range(UNIT_BANKS)]
                for c, xt in enumerate(banks):
                    fresh.append((first + 2 * c, group_units(xt)))
                    inverse_rms(due)
                normalise_waiting(1)
                quantise_units(*fresh.pop(0))
                normalise_waiting(0)
            elif kind == "q":
                release(GD)
                heavy_banks(Q, (j,))
            elif kind == "Q":
                release(GD)
                heavy_banks(Q, tiles)
            elif kind == "K":
                release(GD)
                heavy_banks(KK, tiles)
            elif kind == "V" and j < BLOCKS - 1:
                release(GD)
                values = []
                for i, (m, half) in enumerate([(m, half) for m in tiles for half in range(HALVES)]):
                    if VSL(j, i):
                        values.append(light_on_scalar(m, half))
                        if i == VF:
                            normalise_waiting(0)
                    else:
                        if i <= VF:
                            normalise_waiting(0)
                        v_on_vector(m, half, multiply(m, V, half))
                clock[0] += 3
                release(GD)
                for m, half, value in values:
                    nc.gpsimd.tensor_tensor(out=value[:], in0=value[:], in1=bias_of(V, half), op=ALU.add)
                late_v.extend(values)
            else:
                for item in TAIL:
                    if item == "n":
                        normalise_waiting(max(0, len(waiting) - 1))
                    elif item == "s":
                        release(0)
                    elif item == "r":
                        inverse_rms(due)
                    elif item[0] == "k":
                        m, half = tiles[int(item[1])], int(item[2])
                        heavy_bank(m, KK, half)
                    elif item[0] == "v":
                        m, half = tiles[int(item[1])], int(item[2])
                        v_on_vector(m, half, multiply(m, V, half))
                    elif item[0] == "w":
                        m, half = tiles[int(item[1])], int(item[2])
                        slowv = light_on_scalar(m, half)
                        nc.gpsimd.tensor_tensor(out=slowv[2][:], in0=slowv[2][:], in1=bias_of(V, half), op=ALU.add)
                    elif item[0] == "x":
                        nc.sync.dma_start(out=out_rows(slowv[0], V, slowv[1]), in_=slowv[2][:])
